import numpy as np
import ml_dtypes


BF16 = ml_dtypes.bfloat16


def bf(x):
    return np.asarray(x, np.float32).astype(BF16)


def f64(x):
    return np.asarray(x).astype(np.float64)


E2M1 = np.array([0.0, 0.5, 1.0, 1.5, 2.0, 3.0, 4.0, 6.0, -0.0, -0.5, -1.0, -1.5, -2.0, -3.0, -4.0, -6.0])


def pack_weight(w, fmt):
    k, n = w.shape
    w = f64(bf(w)).reshape(k // 32, 32, n)
    amax = np.abs(w).max(1)
    if fmt == "e4m3":
        byte = np.frexp(amax)[1] - 1 + 127 - 7
    else:
        mant, ex = np.frexp(amax / 6.0)
        byte = np.where(mant > 0.5, ex, ex - 1) + 127
    byte = np.clip(np.where(amax > 0, byte, 1), 1, 254)
    scaled = (w * np.exp2(127.0 - byte)[:, None, :]).reshape(k, n).astype(np.float32)
    by_word = np.ascontiguousarray(scaled.reshape(k // 512, 128, 4, n).transpose(0, 1, 3, 2))
    if fmt == "e4m3":
        words = by_word.astype(ml_dtypes.float8_e4m3fn).view(np.uint8)
    else:
        c = by_word.astype(ml_dtypes.float4_e2m1fn).view(np.uint8) & 0xF
        words = c[..., 0::2] | (c[..., 1::2] << 4)
    return np.ascontiguousarray(words), np.ascontiguousarray(byte.astype(np.uint8).reshape(k // 512, 16, n))


def unpack_weight(words, scales, fmt):
    g, p, n, _ = words.shape
    if fmt == "e4m3":
        vals = np.ascontiguousarray(words).view(ml_dtypes.float8_e4m3fn).astype(np.float64)
    else:
        nib = np.empty((g, p, n, 4), np.uint8)
        nib[..., 0::2] = words & 0xF
        nib[..., 1::2] = words >> 4
        vals = E2M1[nib]
    vals = vals * np.repeat(np.exp2(scales.astype(np.float64) - 127.0), 8, axis=1)[..., None]
    return vals.transpose(0, 1, 3, 2).reshape(g * 512, n)

def pack4(w):
    words, scales = pack_weight(w, "e2m1")
    return words.reshape(words.shape[0], 128, -1), scales


def unpack4(words, scales):
    return unpack_weight(words.reshape(words.shape[0], 128, -1, 2), scales, "e2m1")


def kspread(k):
    return np.exp2(np.repeat(np.random.randint(-6, 7, k // 32), 32).astype(np.float64))


B, T, D, H, HD = 2, 512, 1536, 8, 128
E = H * HD
HALF = HD // 2


def rotate_half(u):
    return np.concatenate((-u[..., HALF:], u[..., :HALF]), axis=-1)


def setup_inputs():
    s = kspread(D)
    x = np.random.standard_normal((B, T, D)) * s
    x_words, x_scales = pack4(np.ascontiguousarray(x.reshape(B * T, D).T))
    rope_cos = bf(np.random.random_sample((1, 1, T, HD)))
    rope_sin = bf(np.random.random_sample((1, 1, T, HD)))
    w = np.random.standard_normal((3 * E, D)) / np.sqrt(D) / s[None, :]
    words, scales = pack4(np.ascontiguousarray(w.T))
    qkv_b = bf(np.random.standard_normal(3 * E) * 0.3)
    return {"x_words": x_words,
            "x_scales": x_scales,
            "rope_cos": rope_cos,
            "rope_sin": rope_sin,
            "qkv_w_words": words,
            "qkv_w_scales": scales,
            "qkv_b": qkv_b}


def reference(x_words, x_scales, rope_cos, rope_sin, qkv_w_words, qkv_w_scales, qkv_b):
    x = unpack4(x_words, x_scales).T.reshape(B, T, D)
    qkv = (x @ unpack4(qkv_w_words, qkv_w_scales)) + f64(qkv_b)
    qkv = qkv.reshape(B, T, 3, H, HD).transpose(2, 0, 3, 1, 4)
    q, k, v = qkv[0], qkv[1], qkv[2]
    cos = f64(rope_cos)[:, :, :T, :]
    sin = f64(rope_sin)[:, :, :T, :]
    q_rot = q * cos + rotate_half(q) * sin
    k_rot = k * cos + rotate_half(k) * sin
    return q_rot, k_rot, v

@@ -1,0 +1,211 @@
+from contextlib import ExitStack
+
+import concourse.mybir as mybir
+from concourse.masks import make_identity
+
+FLOPS = 2 * 1024 * 1536 * 3072
+
+F32 = mybir.dt.float32
+BF16 = mybir.dt.bfloat16
+U8 = mybir.dt.uint8
+I32 = mybir.dt.int32
+FP4X4 = mybir.dt.float4_e2m1fn_x4
+ALU = mybir.AluOpType
+ACT = mybir.ActivationFunctionType
+
+P = 128
+PASSES = 3
+BATCH = 2
+TOK = 512
+HD = 128
+HALF = 64
+HEADS = 8
+SLOTS = 4
+ROUND = 4
+PAIR = 2
+PART = 512
+V_PER_ROUND = (1, 1, 1, 1, 1, 1, 1, 1)
+W_ORDER = (0, 4, 1, 2, 3, 5)
+
+
+def tile_causalselfattention_pa_kernel(
+    tc, x_words, x_scales, rope_cos, rope_sin, qkv_w_words, qkv_w_scales, qkv_b, out_0, out_1, out_2
+):
+    nc = tc.nc
+    with ExitStack() as ctx:
+        ctx.enter_context(tc.manual_schedule())
+        keep = ctx.enter_context(tc.tile_pool(name="keep", bufs=1))
+        work = ctx.enter_context(tc.tile_pool(name="work", bufs=4))
+        psum = ctx.enter_context(tc.psum_pool(name="psum", bufs=8))
+
+        def operand_tiles(label):
+            codes = keep.tile([P, PASSES, 2 * PART], U8, name=label + "_codes", align_bytes=64)
+            plane = keep.tile([P, PASSES, PART], U8, name=label + "_plane", align_bytes=64)
+            nc.vector.memset(plane[:].bitcast(I32), 0)
+            return codes, plane
+
+        def load_codes(op, words, c0):
+            nc.sync.dma_start(
+                out=op[0][:].bitcast(I32),
+                in_=words[:, :, 2 * c0 : 2 * (c0 + PART)].rearrange("g p n -> p g n").bitcast(I32),
+            )
+
+        def load_scales(op, scales, c0):
+            for q in range(4):
+                nc.sync.dma_start(
+                    out=op[1][32 * q : 32 * q + 4, :, :].bitcast(I32),
+                    in_=scales[:, 4 * q : 4 * q + 4, c0 : c0 + PART].rearrange("g r n -> r g n").bitcast(I32),
+                )
+
+        b_rows = keep.tile([P, P], BF16, name="b_rows")
+        nc.vector.memset(b_rows[:], 0.0)
+        b_line = keep.tile([P, HEADS * HD], BF16, name="b_line")
+        nc.vector.memset(b_line[:], 0.0)
+        x_ops = {}
+        w_ops = {}
+        x_ops[0] = operand_tiles("x0")
+        w_ops[W_ORDER[0]] = operand_tiles("w%d" % W_ORDER[0])
+        warm = keep.tile([P, 1], F32, name="warm")
+        warm_out = keep.tile([P, 1], F32, name="warm_out")
+        nc.vector.memset(warm[:], 0.0)
+        ones = keep.tile([P, P], BF16, name="ones")
+        nc.vector.memset(ones[:], 1.0)
+        x_ops[1] = operand_tiles("x1")
+        for part in W_ORDER[1:]:
+            w_ops[part] = operand_tiles("w%d" % part)
+
+        cos = keep.tile([P, SLOTS, HD], BF16, name="cos")
+        sin = keep.tile([P, SLOTS, HD], BF16, name="sin")
+        nc.scalar.dma_start(out=b_rows[0 : 2 * HEADS, :], in_=qkv_b[0 : 2 * HEADS * HD].rearrange("(c d) -> c d", d=HD))
+        nc.scalar.dma_start(
+            out=b_line[0:1, :], in_=qkv_b[2 * HEADS * HD : 3 * HEADS * HD].rearrange("(o n) -> o n", o=1)
+        )
+        nc.scalar.dma_start(out=cos[:], in_=rope_cos[0, 0].rearrange("(p s) d -> p s d", s=SLOTS))
+        nc.scalar.dma_start(out=sin[:], in_=rope_sin[0, 0].rearrange("(p s) d -> p s d", s=SLOTS))
+        nc.scalar.activation(out=warm_out[:], in_=warm[:], func=ACT.Identity, bias=0.0, scale=1.0)
+
+        load_codes(x_ops[0], x_words, 0)
+        load_codes(w_ops[W_ORDER[0]], qkv_w_words, W_ORDER[0] * PART)
+        load_scales(x_ops[0], x_scales, 0)
+        load_scales(w_ops[W_ORDER[0]], qkv_w_scales, W_ORDER[0] * PART)
+        load_codes(x_ops[1], x_words, TOK)
+        load_scales(x_ops[1], x_scales, TOK)
+        for part in W_ORDER[1:]:
+            load_codes(w_ops[part], qkv_w_words, part * PART)
+            load_scales(w_ops[part], qkv_w_scales, part * PART)
+
+        ident = keep.tile([P, P], F32, name="ident")
+        make_identity(nc, ident[:])
+
+        b_rows_f = keep.tile([P, P], F32, name="b_rows_f")
+        nc.vector.tensor_copy(out=b_rows_f[:], in_=b_rows[:])
+        b_t = psum.tile([P, P], F32, tag="bank")
+        nc.tensor.transpose(out=b_t[:], in_=b_rows_f[:], identity=ident[:])
+        b_col = keep.tile([P, 2 * HEADS], F32, name="b_col")
+        nc.vector.tensor_copy(out=b_col[:], in_=b_t[:, 0 : 2 * HEADS])
+        b_v = keep.tile([P, HEADS * HD], F32, name="b_v")
+        for cb in range(2):
+            spread = psum.tile([P, PART], F32, tag="bank")
+            nc.tensor.matmul(out=spread[:], lhsT=ones[:], rhs=b_line[:, cb * PART : (cb + 1) * PART], start=True, stop=True)
+            nc.vector.tensor_copy(out=b_v[:, cb * PART : (cb + 1) * PART], in_=spread[:])
+        nc.vector.tensor_scalar_mul(out=sin[:, :, 0:HALF], in0=sin[:, :, 0:HALF], scalar1=-1.0)
+
+        def project(acc, l_op, l0, r_op, r0):
+            for g in range(PASSES):
+                nc.tensor.matmul_mx(
+                    out=acc,
+                    lhsT=l_op[0][:, g, 2 * l0 : 2 * (l0 + P)].bitcast(FP4X4),
+                    lhsT_scale=l_op[1][:, g, l0 : l0 + P],
+                    rhs=r_op[0][:, g, 2 * r0 : 2 * (r0 + PART)].bitcast(FP4X4),
+                    rhs_scale=r_op[1][:, g, r0 : r0 + PART],
+                    start=(g == 0),
+                    stop=(g == PASSES - 1),
+                )
+
+        def qk_project(b, jh):
+            acc = psum.tile([P, TOK], F32, tag="bank")
+            project(acc[:], w_ops[jh * HD // PART], jh * HD % PART, x_ops[b], 0)
+            u = work.tile([P, SLOTS, P], F32, tag="u", bufs=2 * ROUND)
+            nc.scalar.activation(
+                out=u[:],
+                in_=acc[:].rearrange("c (p s) -> c s p", s=SLOTS),
+                func=ACT.Identity,
+                bias=b_col[:, jh : jh + 1],
+                scale=1.0,
+            )
+            return u
+
+        def to_tokens(u):
+            ut = psum.tile([P, SLOTS, HD], F32, tag="bank")
+            for s in range(SLOTS):
+                nc.tensor.transpose(out=ut[:, s, :], in_=u[:, s, :], identity=ident[:])
+            return ut
+
+        def rope(ut, a, r):
+            nc.vector.tensor_tensor(out=a, in0=ut[:], in1=cos[:], op=ALU.mult)
+            nc.vector.tensor_tensor(out=r[:, :, 0:HALF], in0=ut[:, :, HALF:HD], in1=sin[:, :, 0:HALF], op=ALU.mult)
+            nc.vector.tensor_tensor(out=r[:, :, HALF:HD], in0=ut[:, :, 0:HALF], in1=sin[:, :, HALF:HD], op=ALU.mult)
+
+        def v_project(tb, cb):
+            acc = psum.tile([P, PART], F32, tag="bank")
+            project(acc[:], x_ops[tb // 4], (tb % 4) * P, w_ops[4 + cb], 0)
+            return acc
+
+        def v_finish(acc, tb, cb, queue):
+            o = work.tile([P, 4, HD], F32, tag="ov", bufs=8)
+            nc.vector.tensor_tensor(
+                out=o[:].rearrange("p h d -> p (h d)"), in0=acc[:], in1=b_v[:, cb * PART : (cb + 1) * PART], op=ALU.add
+            )
+            t0 = (tb % 4) * P
+            queue.dma_start(
+                out=out_2[tb // 4, 4 * cb : 4 * cb + 4, t0 : t0 + P, :].rearrange("h p d -> p h d"), in_=o[:]
+            )
+
+        rounds = [(b, [4 * c + i for i in range(ROUND)]) for c in range(2 * HEADS // ROUND) for b in range(BATCH)]
+        v_units = [(tb, cb) for cb in range(2) for tb in range(8)]
+        n_early = sum(V_PER_ROUND)
+
+        v_next = 0
+        for r in range(len(rounds)):
+            last = r == len(rounds) - 1
+            b, heads = rounds[r]
+            us = [qk_project(b, jh) for jh in heads]
+            uts = [to_tokens(u) for u in us]
+            v_accs = []
+            n_v = len(v_units) - n_early if last else V_PER_ROUND[r]
+            for i in range(n_v):
+                v_accs.append((v_project(*v_units[v_next]), v_units[v_next]))
+                v_next += 1
+                if len(v_accs) > 3:
+                    break
+            for i0 in range(0, ROUND, PAIR):
+                a2 = work.tile([P, PAIR, SLOTS, HD], F32, tag="a2", bufs=6)
+                r2 = work.tile([P, PAIR, SLOTS, HD], F32, tag="r2", bufs=6)
+                o2 = work.tile([P, PAIR, SLOTS, HD], F32, tag="o2", bufs=4)
+                for i in range(PAIR):
+                    rope(uts[i0 + i], a2[:, i], r2[:, i])
+                nc.gpsimd.tensor_tensor(
+                    out=o2[:].rearrange("p u s d -> p (u s d)"),
+                    in0=a2[:].rearrange("p u s d -> p (u s d)"),
+                    in1=r2[:].rearrange("p u s d -> p (u s d)"),
+                    op=ALU.add,
+                )
+                jh = heads[i0]
+                dst = out_0 if jh < HEADS else out_1
+                h = jh % HEADS
+                nc.sync.dma_start(
+                    out=dst[b, h : h + PAIR].rearrange("u (p s) d -> p u (s d)", s=SLOTS),
+                    in_=o2[:].rearrange("p u s d -> p u (s d)"),
+                )
+                for i in range(2 if last else 1):
+                    if v_accs:
+                        acc, unit = v_accs.pop(0)
+                        v_finish(acc, unit[0], unit[1], nc.scalar if last else nc.sync)
+        pending = []
+        while v_next < len(v_units) or pending:
+            if v_next < len(v_units):
+                pending.append((v_project(*v_units[v_next]), v_units[v_next]))
+                v_next += 1
+            if len(pending) > 2 or v_next >= len(v_units):
+                acc, unit = pending.pop(0)
+                v_finish(acc, unit[0], unit[1], nc.scalar)

@@ -23,9 +23,12 @@ HEADS = 8
 SLOTS = 4
 ROUND = 4
 PAIR = 2
-PART = 512
-V_PER_ROUND = (1, 1, 1, 1, 1, 1, 1, 1)
+BANK = 512
+BANKS = 8
+V0 = 2 * HEADS * HD
+V_PER_ROUND = (1, 1, 1, 1, 1, 1, 0, 0)
 W_ORDER = (0, 4, 1, 2, 3, 5)
+WARM = 10
 
 
 def tile_causalselfattention_pa_kernel(
@@ -36,66 +39,74 @@ def tile_causalselfattention_pa_kernel(
         ctx.enter_context(tc.manual_schedule())
         keep = ctx.enter_context(tc.tile_pool(name="keep", bufs=1))
         work = ctx.enter_context(tc.tile_pool(name="work", bufs=4))
-        psum = ctx.enter_context(tc.psum_pool(name="psum", bufs=8))
+        psum = ctx.enter_context(tc.psum_pool(name="psum", bufs=BANKS))
 
-        def operand_tiles(label):
-            codes = keep.tile([P, PASSES, 2 * PART], U8, name=label + "_codes", align_bytes=64)
-            plane = keep.tile([P, PASSES, PART], U8, name=label + "_plane", align_bytes=64)
-            nc.vector.memset(plane[:].bitcast(I32), 0)
-            return codes, plane
+        def operand(label, words, scales, lo, fill):
+            codes = keep.tile([P, PASSES, 2 * BANK], U8, name=label + "_codes", align_bytes=64)
+            plane = keep.tile([P, PASSES, BANK], U8, name=label + "_plane", align_bytes=64)
+            if fill == "vector":
+                nc.vector.memset(plane[:].bitcast(I32), 0)
+            else:
+                nc.gpsimd.memset(plane[:].bitcast(F32), 0.0)
+            return {"codes": codes, "plane": plane, "words": words, "scales": scales, "lo": lo}
 
-        def load_codes(op, words, c0):
+        def load_codes(op):
             nc.sync.dma_start(
-                out=op[0][:].bitcast(I32),
-                in_=words[:, :, 2 * c0 : 2 * (c0 + PART)].rearrange("g p n -> p g n").bitcast(I32),
+                out=op["codes"][:].bitcast(I32),
+                in_=op["words"][:, :, 2 * op["lo"] : 2 * (op["lo"] + BANK)].rearrange("g p n -> p g n").bitcast(I32),
             )
 
-        def load_scales(op, scales, c0):
+        def load_scales(op):
             for q in range(4):
                 nc.sync.dma_start(
-                    out=op[1][32 * q : 32 * q + 4, :, :].bitcast(I32),
-                    in_=scales[:, 4 * q : 4 * q + 4, c0 : c0 + PART].rearrange("g r n -> r g n").bitcast(I32),
+                    out=op["plane"][32 * q : 32 * q + 4, :, :].bitcast(I32),
+                    in_=op["scales"][:, 4 * q : 4 * q + 4, op["lo"] : op["lo"] + BANK]
+                    .rearrange("g r n -> r g n")
+                    .bitcast(I32),
                 )
 
-        b_rows = keep.tile([P, P], BF16, name="b_rows")
-        nc.vector.memset(b_rows[:], 0.0)
-        b_line = keep.tile([P, HEADS * HD], BF16, name="b_line")
-        nc.vector.memset(b_line[:], 0.0)
         x_ops = {}
         w_ops = {}
-        x_ops[0] = operand_tiles("x0")
-        w_ops[W_ORDER[0]] = operand_tiles("w%d" % W_ORDER[0])
+        x_ops[0] = operand("x0", x_words, x_scales, 0, "vector")
+        w_ops[W_ORDER[0]] = operand("w%d" % W_ORDER[0], qkv_w_words, qkv_w_scales, W_ORDER[0] * BANK, "gpsimd")
+        ones = keep.tile([P, BANK], BF16, name="ones")
+        nc.vector.memset(ones[:], 1.0)
+        b_rows = keep.tile([P, P], BF16, name="b_rows")
+        nc.vector.memset(b_rows[:], 0.0)
         warm = keep.tile([P, 1], F32, name="warm")
         warm_out = keep.tile([P, 1], F32, name="warm_out")
         nc.vector.memset(warm[:], 0.0)
-        ones = keep.tile([P, P], BF16, name="ones")
-        nc.vector.memset(ones[:], 1.0)
-        x_ops[1] = operand_tiles("x1")
-        for part in W_ORDER[1:]:
-            w_ops[part] = operand_tiles("w%d" % part)
+        ident = keep.tile([P, P], F32, name="ident")
+        make_identity(nc, ident[:])
+        x_ops[1] = operand("x1", x_words, x_scales, TOK, "vector")
+        b_line = keep.tile([P, HEADS * HD], BF16, name="b_line")
+        nc.vector.memset(b_line[:], 0.0)
+        for i in W_ORDER[1:]:
+            w_ops[i] = operand("w%d" % i, qkv_w_words, qkv_w_scales, i * BANK, "gpsimd")
+
+        nc.scalar.dma_start(out=b_rows[0 : 2 * HEADS, :], in_=qkv_b[0:V0].rearrange("(c d) -> c d", d=HD))
+        nc.scalar.activation(out=warm_out[:], in_=warm[:], func=ACT.Identity, bias=0.0, scale=1.0)
+        nc.scalar.dma_start(out=b_line[0:1, :], in_=qkv_b[V0 : V0 + HEADS * HD].rearrange("(o n) -> o n", o=1))
 
         cos = keep.tile([P, SLOTS, HD], BF16, name="cos")
         sin = keep.tile([P, SLOTS, HD], BF16, name="sin")
-        nc.scalar.dma_start(out=b_rows[0 : 2 * HEADS, :], in_=qkv_b[0 : 2 * HEADS * HD].rearrange("(c d) -> c d", d=HD))
-        nc.scalar.dma_start(
-            out=b_line[0:1, :], in_=qkv_b[2 * HEADS * HD : 3 * HEADS * HD].rearrange("(o n) -> o n", o=1)
-        )
-        nc.scalar.dma_start(out=cos[:], in_=rope_cos[0, 0].rearrange("(p s) d -> p s d", s=SLOTS))
-        nc.scalar.dma_start(out=sin[:], in_=rope_sin[0, 0].rearrange("(p s) d -> p s d", s=SLOTS))
-        nc.scalar.activation(out=warm_out[:], in_=warm[:], func=ACT.Identity, bias=0.0, scale=1.0)
+        load_codes(x_ops[0])
+        load_codes(w_ops[W_ORDER[0]])
+        load_scales(x_ops[0])
+        load_scales(w_ops[W_ORDER[0]])
+        nc.sync.dma_start(out=cos[:], in_=rope_cos[0, 0].rearrange("(p s) d -> p s d", s=SLOTS))
+        nc.sync.dma_start(out=sin[:], in_=rope_sin[0, 0].rearrange("(p s) d -> p s d", s=SLOTS))
+        load_codes(w_ops[W_ORDER[1]])
+        load_scales(w_ops[W_ORDER[1]])
+        load_codes(x_ops[1])
+        load_scales(x_ops[1])
+        for i in W_ORDER[2:]:
+            load_codes(w_ops[i])
+            load_scales(w_ops[i])
 
-        load_codes(x_ops[0], x_words, 0)
-        load_codes(w_ops[W_ORDER[0]], qkv_w_words, W_ORDER[0] * PART)
-        load_scales(x_ops[0], x_scales, 0)
-        load_scales(w_ops[W_ORDER[0]], qkv_w_scales, W_ORDER[0] * PART)
-        load_codes(x_ops[1], x_words, TOK)
-        load_scales(x_ops[1], x_scales, TOK)
-        for part in W_ORDER[1:]:
-            load_codes(w_ops[part], qkv_w_words, part * PART)
-            load_scales(w_ops[part], qkv_w_scales, part * PART)
-
-        ident = keep.tile([P, P], F32, name="ident")
-        make_identity(nc, ident[:])
+        heat = psum.tile([P, BANK], F32, tag="bank")
+        for i in range(WARM):
+            nc.tensor.matmul(out=heat[:], lhsT=ones[:, 0:P], rhs=ones[:], start=True, stop=True)
 
         b_rows_f = keep.tile([P, P], F32, name="b_rows_f")
         nc.vector.tensor_copy(out=b_rows_f[:], in_=b_rows[:])
@@ -103,28 +114,34 @@ def tile_causalselfattention_pa_kernel(
         nc.tensor.transpose(out=b_t[:], in_=b_rows_f[:], identity=ident[:])
         b_col = keep.tile([P, 2 * HEADS], F32, name="b_col")
         nc.vector.tensor_copy(out=b_col[:], in_=b_t[:, 0 : 2 * HEADS])
-        b_v = keep.tile([P, HEADS * HD], F32, name="b_v")
-        for cb in range(2):
-            spread = psum.tile([P, PART], F32, tag="bank")
-            nc.tensor.matmul(out=spread[:], lhsT=ones[:], rhs=b_line[:, cb * PART : (cb + 1) * PART], start=True, stop=True)
-            nc.vector.tensor_copy(out=b_v[:, cb * PART : (cb + 1) * PART], in_=spread[:])
         nc.vector.tensor_scalar_mul(out=sin[:, :, 0:HALF], in0=sin[:, :, 0:HALF], scalar1=-1.0)
+        b_v = keep.tile([P, HEADS * HD], F32, name="b_v")
 
-        def project(acc, l_op, l0, r_op, r0):
+        def spread_v_bias():
+            for cb in range(2):
+                spread = psum.tile([P, BANK], F32, tag="bank")
+                nc.tensor.matmul(
+                    out=spread[:], lhsT=ones[:, 0:P], rhs=b_line[:, cb * BANK : (cb + 1) * BANK], start=True, stop=True
+                )
+                nc.scalar.activation(
+                    out=b_v[:, cb * BANK : (cb + 1) * BANK], in_=spread[:], func=ACT.Identity, bias=0.0, scale=1.0
+                )
+
+        def project(acc, l_op, l0, r_op):
             for g in range(PASSES):
                 nc.tensor.matmul_mx(
                     out=acc,
-                    lhsT=l_op[0][:, g, 2 * l0 : 2 * (l0 + P)].bitcast(FP4X4),
-                    lhsT_scale=l_op[1][:, g, l0 : l0 + P],
-                    rhs=r_op[0][:, g, 2 * r0 : 2 * (r0 + PART)].bitcast(FP4X4),
-                    rhs_scale=r_op[1][:, g, r0 : r0 + PART],
+                    lhsT=l_op["codes"][:, g, 2 * l0 : 2 * (l0 + P)].bitcast(FP4X4),
+                    lhsT_scale=l_op["plane"][:, g, l0 : l0 + P],
+                    rhs=r_op["codes"][:, g, :].bitcast(FP4X4),
+                    rhs_scale=r_op["plane"][:, g, :],
                     start=(g == 0),
                     stop=(g == PASSES - 1),
                 )
 
         def qk_project(b, jh):
             acc = psum.tile([P, TOK], F32, tag="bank")
-            project(acc[:], w_ops[jh * HD // PART], jh * HD % PART, x_ops[b], 0)
+            project(acc[:], w_ops[jh * HD // BANK], jh * HD % BANK, x_ops[b])
             u = work.tile([P, SLOTS, P], F32, tag="u", bufs=2 * ROUND)
             nc.scalar.activation(
                 out=u[:],
@@ -146,15 +163,35 @@ def tile_causalselfattention_pa_kernel(
             nc.vector.tensor_tensor(out=r[:, :, 0:HALF], in0=ut[:, :, HALF:HD], in1=sin[:, :, 0:HALF], op=ALU.mult)
             nc.vector.tensor_tensor(out=r[:, :, HALF:HD], in0=ut[:, :, 0:HALF], in1=sin[:, :, HALF:HD], op=ALU.mult)
 
+        def rope_heads(b, heads, uts):
+            n = len(heads)
+            a2 = work.tile([P, PAIR, SLOTS, HD], F32, tag="a2", bufs=6)
+            r2 = work.tile([P, PAIR, SLOTS, HD], F32, tag="r2", bufs=6)
+            o2 = work.tile([P, PAIR, SLOTS, HD], F32, tag="o2", bufs=4)
+            for i in range(n):
+                rope(uts[i], a2[:, i], r2[:, i])
+            nc.gpsimd.tensor_tensor(
+                out=o2[:, 0:n].rearrange("p u s d -> p (u s d)"),
+                in0=a2[:, 0:n].rearrange("p u s d -> p (u s d)"),
+                in1=r2[:, 0:n].rearrange("p u s d -> p (u s d)"),
+                op=ALU.add,
+            )
+            dst = out_0 if heads[0] < HEADS else out_1
+            h = heads[0] % HEADS
+            nc.sync.dma_start(
+                out=dst[b, h : h + n].rearrange("u (p s) d -> p u (s d)", s=SLOTS),
+                in_=o2[:, 0:n].rearrange("p u s d -> p u (s d)"),
+            )
+
         def v_project(tb, cb):
-            acc = psum.tile([P, PART], F32, tag="bank")
-            project(acc[:], x_ops[tb // 4], (tb % 4) * P, w_ops[4 + cb], 0)
+            acc = psum.tile([P, BANK], F32, tag="bank")
+            project(acc[:], x_ops[tb // 4], (tb % 4) * P, w_ops[4 + cb])
             return acc
 
         def v_finish(acc, tb, cb, queue):
             o = work.tile([P, 4, HD], F32, tag="ov", bufs=8)
             nc.vector.tensor_tensor(
-                out=o[:].rearrange("p h d -> p (h d)"), in0=acc[:], in1=b_v[:, cb * PART : (cb + 1) * PART], op=ALU.add
+                out=o[:].rearrange("p h d -> p (h d)"), in0=acc[:], in1=b_v[:, cb * BANK : (cb + 1) * BANK], op=ALU.add
             )
             t0 = (tb % 4) * P
             queue.dma_start(
@@ -163,49 +200,48 @@ def tile_causalselfattention_pa_kernel(
 
         rounds = [(b, [4 * c + i for i in range(ROUND)]) for c in range(2 * HEADS // ROUND) for b in range(BATCH)]
         v_units = [(tb, cb) for cb in range(2) for tb in range(8)]
-        n_early = sum(V_PER_ROUND)
 
-        v_next = 0
-        for r in range(len(rounds)):
-            last = r == len(rounds) - 1
+        for r in range(len(rounds) - 1):
             b, heads = rounds[r]
             us = [qk_project(b, jh) for jh in heads]
+            if r == 0:
+                spread_v_bias()
             uts = [to_tokens(u) for u in us]
             v_accs = []
-            n_v = len(v_units) - n_early if last else V_PER_ROUND[r]
-            for i in range(n_v):
-                v_accs.append((v_project(*v_units[v_next]), v_units[v_next]))
-                v_next += 1
-                if len(v_accs) > 3:
-                    break
+            for i in range(V_PER_ROUND[r]):
+                unit = v_units.pop(0)
+                v_accs.append((v_project(*unit), unit))
             for i0 in range(0, ROUND, PAIR):
-                a2 = work.tile([P, PAIR, SLOTS, HD], F32, tag="a2", bufs=6)
-                r2 = work.tile([P, PAIR, SLOTS, HD], F32, tag="r2", bufs=6)
-                o2 = work.tile([P, PAIR, SLOTS, HD], F32, tag="o2", bufs=4)
-                for i in range(PAIR):
-                    rope(uts[i0 + i], a2[:, i], r2[:, i])
-                nc.gpsimd.tensor_tensor(
-                    out=o2[:].rearrange("p u s d -> p (u s d)"),
-                    in0=a2[:].rearrange("p u s d -> p (u s d)"),
-                    in1=r2[:].rearrange("p u s d -> p (u s d)"),
-                    op=ALU.add,
-                )
-                jh = heads[i0]
-                dst = out_0 if jh < HEADS else out_1
-                h = jh % HEADS
-                nc.sync.dma_start(
-                    out=dst[b, h : h + PAIR].rearrange("u (p s) d -> p u (s d)", s=SLOTS),
-                    in_=o2[:].rearrange("p u s d -> p u (s d)"),
-                )
-                for i in range(2 if last else 1):
-                    if v_accs:
-                        acc, unit = v_accs.pop(0)
-                        v_finish(acc, unit[0], unit[1], nc.scalar if last else nc.sync)
-        pending = []
-        while v_next < len(v_units) or pending:
-            if v_next < len(v_units):
-                pending.append((v_project(*v_units[v_next]), v_units[v_next]))
-                v_next += 1
-            if len(pending) > 2 or v_next >= len(v_units):
-                acc, unit = pending.pop(0)
-                v_finish(acc, unit[0], unit[1], nc.scalar)
+                rope_heads(b, heads[i0 : i0 + PAIR], uts[i0 : i0 + PAIR])
+                if v_accs:
+                    acc, unit = v_accs.pop(0)
+                    v_finish(acc, unit[0], unit[1], nc.sync)
+
+        b, heads = rounds[-1]
+        us = [qk_project(b, jh) for jh in heads]
+        uts = [to_tokens(u) for u in us]
+        state = {"live": ROUND}
+        v_accs = []
+
+        def fill_banks():
+            while v_units and state["live"] < BANKS:
+                unit = v_units.pop(0)
+                v_accs.append((v_project(*unit), unit))
+                state["live"] += 1
+
+        def finish_v(n):
+            for i in range(n):
+                if v_accs:
+                    acc, unit = v_accs.pop(0)
+                    v_finish(acc, unit[0], unit[1], nc.scalar)
+                    state["live"] -= 1
+                    fill_banks()
+
+        fill_banks()
+        for i in range(ROUND):
+            rope_heads(b, heads[i : i + 1], uts[i : i + 1])
+            state["live"] -= 1
+            fill_banks()
+            if i > 0:
+                finish_v(2)
+        finish_v(len(v_units) + len(v_accs))

@@ -26,7 +26,9 @@ PAIR = 2
 BANK = 512
 BANKS = 8
 V0 = 2 * HEADS * HD
-V_PER_ROUND = (1, 1, 1, 1, 1, 1, 0, 0)
+ROUND_SIZES = (4, 4, 4, 4, 4, 4, 4)
+V_PER_ROUND = (1, 1, 1, 1, 1, 1, 0)
+END_V = 2
 W_ORDER = (0, 4, 1, 2, 3, 5)
 WARM = 10
 
@@ -50,10 +52,10 @@ def tile_causalselfattention_pa_kernel(
                 nc.gpsimd.memset(plane[:].bitcast(F32), 0.0)
             return {"codes": codes, "plane": plane, "words": words, "scales": scales, "lo": lo}
 
-        def load_codes(op):
+        def load_codes(op, g0=0, g1=PASSES):
             nc.sync.dma_start(
-                out=op["codes"][:].bitcast(I32),
-                in_=op["words"][:, :, 2 * op["lo"] : 2 * (op["lo"] + BANK)].rearrange("g p n -> p g n").bitcast(I32),
+                out=op["codes"][:, g0:g1, :].bitcast(I32),
+                in_=op["words"][g0:g1, :, 2 * op["lo"] : 2 * (op["lo"] + BANK)].rearrange("g p n -> p g n").bitcast(I32),
             )
 
         def load_scales(op):
@@ -65,42 +67,53 @@ def tile_causalselfattention_pa_kernel(
                     .bitcast(I32),
                 )
 
+        def bias_line(line, lo):
+            nc.scalar.dma_start(out=line[0:1, :], in_=qkv_b[lo : lo + BANK].rearrange("(o n) -> o n", o=1))
+
         x_ops = {}
         w_ops = {}
         x_ops[0] = operand("x0", x_words, x_scales, 0, "vector")
-        w_ops[W_ORDER[0]] = operand("w%d" % W_ORDER[0], qkv_w_words, qkv_w_scales, W_ORDER[0] * BANK, "gpsimd")
-        ones = keep.tile([P, BANK], BF16, name="ones")
-        nc.vector.memset(ones[:], 1.0)
+        w_ops[0] = operand("w0", qkv_w_words, qkv_w_scales, 0, "gpsimd")
+        b_lines = []
+        for i in range(3):
+            line = keep.tile([P, BANK], BF16, name="b_line%d" % i)
+            b_lines.append(line)
+        nc.vector.memset(b_lines[0][:], 0.0)
         b_rows = keep.tile([P, P], BF16, name="b_rows")
         nc.vector.memset(b_rows[:], 0.0)
+        ones = keep.tile([P, BANK], BF16, name="ones")
+        nc.vector.memset(ones[:], 1.0)
         warm = keep.tile([P, 1], F32, name="warm")
         warm_out = keep.tile([P, 1], F32, name="warm_out")
         nc.vector.memset(warm[:], 0.0)
         ident = keep.tile([P, P], F32, name="ident")
         make_identity(nc, ident[:])
         x_ops[1] = operand("x1", x_words, x_scales, TOK, "vector")
-        b_line = keep.tile([P, HEADS * HD], BF16, name="b_line")
-        nc.vector.memset(b_line[:], 0.0)
+        nc.vector.memset(b_lines[1][:], 0.0)
+        nc.vector.memset(b_lines[2][:], 0.0)
         for i in W_ORDER[1:]:
             w_ops[i] = operand("w%d" % i, qkv_w_words, qkv_w_scales, i * BANK, "gpsimd")
-
-        nc.scalar.dma_start(out=b_rows[0 : 2 * HEADS, :], in_=qkv_b[0:V0].rearrange("(c d) -> c d", d=HD))
-        nc.scalar.activation(out=warm_out[:], in_=warm[:], func=ACT.Identity, bias=0.0, scale=1.0)
-        nc.scalar.dma_start(out=b_line[0:1, :], in_=qkv_b[V0 : V0 + HEADS * HD].rearrange("(o n) -> o n", o=1))
-
         cos = keep.tile([P, SLOTS, HD], BF16, name="cos")
         sin = keep.tile([P, SLOTS, HD], BF16, name="sin")
+        cos_n = keep.tile([P, SLOTS, HD], BF16, name="cos_n")
+        sin_n = keep.tile([P, SLOTS, HD], BF16, name="sin_n")
+
+        bias_line(b_lines[0], 0)
+        nc.scalar.dma_start(out=b_rows[0 : 2 * HEADS, :], in_=qkv_b[0:V0].rearrange("(c d) -> c d", d=HD))
+        nc.scalar.activation(out=warm_out[:], in_=warm[:], func=ACT.Identity, bias=0.0, scale=1.0)
+        bias_line(b_lines[1], V0)
+        bias_line(b_lines[2], V0 + BANK)
         load_codes(x_ops[0])
-        load_codes(w_ops[W_ORDER[0]])
+        load_codes(w_ops[0])
         load_scales(x_ops[0])
-        load_scales(w_ops[W_ORDER[0]])
-        nc.sync.dma_start(out=cos[:], in_=rope_cos[0, 0].rearrange("(p s) d -> p s d", s=SLOTS))
-        nc.sync.dma_start(out=sin[:], in_=rope_sin[0, 0].rearrange("(p s) d -> p s d", s=SLOTS))
-        load_codes(w_ops[W_ORDER[1]])
-        load_scales(w_ops[W_ORDER[1]])
+        load_scales(w_ops[0])
+        nc.sync.dma_start(out=cos_n[:], in_=rope_cos[0, 0].rearrange("(t p) d -> p t d", p=P))
+        nc.sync.dma_start(out=sin_n[:], in_=rope_sin[0, 0].rearrange("(t p) d -> p t d", p=P))
         load_codes(x_ops[1])
         load_scales(x_ops[1])
-        for i in W_ORDER[2:]:
+        nc.sync.dma_start(out=cos[:], in_=rope_cos[0, 0].rearrange("(p s) d -> p s d", s=SLOTS))
+        nc.sync.dma_start(out=sin[:], in_=rope_sin[0, 0].rearrange("(p s) d -> p s d", s=SLOTS))
+        for i in W_ORDER[1:]:
             load_codes(w_ops[i])
             load_scales(w_ops[i])
 
@@ -114,18 +127,19 @@ def tile_causalselfattention_pa_kernel(
         nc.tensor.transpose(out=b_t[:], in_=b_rows_f[:], identity=ident[:])
         b_col = keep.tile([P, 2 * HEADS], F32, name="b_col")
         nc.vector.tensor_copy(out=b_col[:], in_=b_t[:, 0 : 2 * HEADS])
-        nc.vector.tensor_scalar_mul(out=sin[:, :, 0:HALF], in0=sin[:, :, 0:HALF], scalar1=-1.0)
-        b_v = keep.tile([P, HEADS * HD], F32, name="b_v")
+        b_free = keep.tile([P, 3 * BANK], F32, name="b_free")
 
-        def spread_v_bias():
-            for cb in range(2):
+        def spread_bias(blocks):
+            for cb in blocks:
                 spread = psum.tile([P, BANK], F32, tag="bank")
                 nc.tensor.matmul(
-                    out=spread[:], lhsT=ones[:, 0:P], rhs=b_line[:, cb * BANK : (cb + 1) * BANK], start=True, stop=True
+                    out=spread[:], lhsT=ones[:, 0:P], rhs=b_lines[cb][:], start=True, stop=True
                 )
                 nc.scalar.activation(
-                    out=b_v[:, cb * BANK : (cb + 1) * BANK], in_=spread[:], func=ACT.Identity, bias=0.0, scale=1.0
+                    out=b_free[:, cb * BANK : (cb + 1) * BANK], in_=spread[:], func=ACT.Identity, bias=0.0, scale=1.0
                 )
+
+        spread_bias([0])
 
         def project(acc, l_op, l0, r_op):
             for g in range(PASSES):
@@ -178,9 +192,9 @@ def tile_causalselfattention_pa_kernel(
             )
             dst = out_0 if heads[0] < HEADS else out_1
             h = heads[0] % HEADS
-            nc.sync.dma_start(
-                out=dst[b, h : h + n].rearrange("u (p s) d -> p u (s d)", s=SLOTS),
-                in_=o2[:, 0:n].rearrange("p u s d -> p u (s d)"),
+            return (
+                dst[b, h : h + n].rearrange("u (p s) d -> p u (s d)", s=SLOTS),
+                o2[:, 0:n].rearrange("p u s d -> p u (s d)"),
             )
 
         def v_project(tb, cb):
@@ -191,36 +205,85 @@ def tile_causalselfattention_pa_kernel(
         def v_finish(acc, tb, cb, queue):
             o = work.tile([P, 4, HD], F32, tag="ov", bufs=8)
             nc.vector.tensor_tensor(
-                out=o[:].rearrange("p h d -> p (h d)"), in0=acc[:], in1=b_v[:, cb * BANK : (cb + 1) * BANK], op=ALU.add
+                out=o[:].rearrange("p h d -> p (h d)"), in0=acc[:], in1=b_free[:, (1 + cb) * BANK : (2 + cb) * BANK], op=ALU.add
             )
             t0 = (tb % 4) * P
             queue.dma_start(
                 out=out_2[tb // 4, 4 * cb : 4 * cb + 4, t0 : t0 + P, :].rearrange("h p d -> p h d"), in_=o[:]
             )
 
-        rounds = [(b, [4 * c + i for i in range(ROUND)]) for c in range(2 * HEADS // ROUND) for b in range(BATCH)]
+        def direct_project(t):
+            acc = psum.tile([P, BANK], F32, tag="bank")
+            project(acc[:], x_ops[0], t * P, w_ops[0])
+            u = work.tile([P, 4, HD], F32, tag="ud", bufs=4)
+            nc.vector.tensor_tensor(out=u[:].rearrange("p h d -> p (h d)"), in0=acc[:], in1=b_free[:, 0:BANK], op=ALU.add)
+            return u
+
+        def direct_rope(u, t, a, r):
+            nc.vector.tensor_tensor(out=a, in0=u[:], in1=cos_n[:, t : t + 1, :].to_broadcast([P, 4, HD]), op=ALU.mult)
+            nc.vector.tensor_tensor(
+                out=r[:, :, 0:HALF],
+                in0=u[:, :, HALF:HD],
+                in1=sin_n[:, t : t + 1, 0:HALF].to_broadcast([P, 4, HALF]),
+                op=ALU.mult,
+            )
+            nc.vector.tensor_tensor(
+                out=r[:, :, HALF:HD],
+                in0=u[:, :, 0:HALF],
+                in1=sin_n[:, t : t + 1, HALF:HD].to_broadcast([P, 4, HALF]),
+                op=ALU.mult,
+            )
+
+        a4 = work.tile([P, SLOTS, 4, HD], F32, tag="a4", bufs=1)
+        r4 = work.tile([P, SLOTS, 4, HD], F32, tag="r4", bufs=1)
+        o4 = work.tile([P, SLOTS, 4, HD], F32, tag="o4", bufs=1)
+        uds = []
+        for t in range(SLOTS + 1):
+            if t < SLOTS:
+                uds.append(direct_project(t))
+            if t == 1:
+                nc.vector.tensor_scalar_mul(out=sin_n[:, :, 0:HALF], in0=sin_n[:, :, 0:HALF], scalar1=-1.0)
+            if t > 0:
+                direct_rope(uds[t - 1], t - 1, a4[:, t - 1], r4[:, t - 1])
+        nc.gpsimd.tensor_tensor(
+            out=o4[:].rearrange("p t h d -> p (t h d)"),
+            in0=a4[:].rearrange("p t h d -> p (t h d)"),
+            in1=r4[:].rearrange("p t h d -> p (t h d)"),
+            op=ALU.add,
+        )
+        for t in range(SLOTS):
+            nc.sync.dma_start(out=out_0[0, 0:4, t * P : (t + 1) * P, :].rearrange("h p d -> p h d"), in_=o4[:, t])
+
+        nc.vector.tensor_scalar_mul(out=sin[:, :, 0:HALF], in0=sin[:, :, 0:HALF], scalar1=-1.0)
+        units = [(b, 4 * c + i) for c in range(2 * HEADS // 4) for b in range(BATCH) for i in range(4)][4:]
+        rounds = []
+        for size in ROUND_SIZES:
+            rounds.append((units[0][0], [jh for b, jh in units[0:size]]))
+            units = units[size:]
         v_units = [(tb, cb) for cb in range(2) for tb in range(8)]
 
         for r in range(len(rounds) - 1):
             b, heads = rounds[r]
             us = [qk_project(b, jh) for jh in heads]
             if r == 0:
-                spread_v_bias()
+                spread_bias([1, 2])
             uts = [to_tokens(u) for u in us]
             v_accs = []
             for i in range(V_PER_ROUND[r]):
                 unit = v_units.pop(0)
                 v_accs.append((v_project(*unit), unit))
-            for i0 in range(0, ROUND, PAIR):
-                rope_heads(b, heads[i0 : i0 + PAIR], uts[i0 : i0 + PAIR])
-                if v_accs:
-                    acc, unit = v_accs.pop(0)
-                    v_finish(acc, unit[0], unit[1], nc.sync)
+            for i0 in range(0, len(heads), PAIR):
+                dst_ap, src_ap = rope_heads(b, heads[i0 : i0 + PAIR], uts[i0 : i0 + PAIR])
+                for i in range(1 if i0 + PAIR < len(heads) else len(v_accs)):
+                    if v_accs:
+                        acc, unit = v_accs.pop(0)
+                        v_finish(acc, unit[0], unit[1], nc.sync)
+                nc.sync.dma_start(out=dst_ap, in_=src_ap)
 
         b, heads = rounds[-1]
         us = [qk_project(b, jh) for jh in heads]
         uts = [to_tokens(u) for u in us]
-        state = {"live": ROUND}
+        state = {"live": len(heads)}
         v_accs = []
 
         def fill_banks():
@@ -238,10 +301,11 @@ def tile_causalselfattention_pa_kernel(
                     fill_banks()
 
         fill_banks()
-        for i in range(ROUND):
-            rope_heads(b, heads[i : i + 1], uts[i : i + 1])
+        for i in range(len(heads)):
+            dst_ap, src_ap = rope_heads(b, heads[i : i + 1], uts[i : i + 1])
+            nc.sync.dma_start(out=dst_ap, in_=src_ap)
             state["live"] -= 1
             fill_banks()
             if i > 0:
-                finish_v(2)
+                finish_v(END_V)
         finish_v(len(v_units) + len(v_accs))

@@ -44,8 +44,8 @@ def tile_causalselfattention_pa_kernel(
         psum = ctx.enter_context(tc.psum_pool(name="psum", bufs=BANKS))
 
         def operand(label, words, scales, lo, fill):
-            codes = keep.tile([P, PASSES, 2 * BANK], U8, name=label + "_codes", align_bytes=64)
-            plane = keep.tile([P, PASSES, BANK], U8, name=label + "_plane", align_bytes=64)
+            codes = keep.tile([P, PASSES, 2 * BANK], U8, name=label + "_codes", align_bytes=256)
+            plane = keep.tile([P, PASSES, BANK], U8, name=label + "_plane", align_bytes=256)
             if fill == "vector":
                 nc.vector.memset(plane[:].bitcast(I32), 0)
             else:

from contextlib import ExitStack

import concourse.mybir as mybir
from concourse.masks import make_identity

FLOPS = 2 * 1024 * 1536 * 3072

F32 = mybir.dt.float32
BF16 = mybir.dt.bfloat16
U8 = mybir.dt.uint8
I32 = mybir.dt.int32
FP4X4 = mybir.dt.float4_e2m1fn_x4
ALU = mybir.AluOpType
ACT = mybir.ActivationFunctionType

P = 128
PASSES = 3
BATCH = 2
TOK = 512
HD = 128
HALF = 64
HEADS = 8
SLOTS = 4
ROUND = 4
PAIR = 2
BANK = 512
BANKS = 8
V0 = 2 * HEADS * HD
ROUND_SIZES = (4, 4, 4, 4, 4, 4, 4)
V_PER_ROUND = (1, 1, 1, 1, 1, 1, 0)
END_V = 2
W_ORDER = (0, 4, 1, 2, 3, 5)
WARM = 10


def tile_causalselfattention_pa_kernel(
    tc, x_words, x_scales, rope_cos, rope_sin, qkv_w_words, qkv_w_scales, qkv_b, out_0, out_1, out_2
):
    nc = tc.nc
    with ExitStack() as ctx:
        ctx.enter_context(tc.manual_schedule())
        keep = ctx.enter_context(tc.tile_pool(name="keep", bufs=1))
        work = ctx.enter_context(tc.tile_pool(name="work", bufs=4))
        psum = ctx.enter_context(tc.psum_pool(name="psum", bufs=BANKS))

        def operand(label, words, scales, lo, fill):
            codes = keep.tile([P, PASSES, 2 * BANK], U8, name=label + "_codes", align_bytes=256)
            plane = keep.tile([P, PASSES, BANK], U8, name=label + "_plane", align_bytes=256)
            if fill == "vector":
                nc.vector.memset(plane[:].bitcast(I32), 0)
            else:
                nc.gpsimd.memset(plane[:].bitcast(F32), 0.0)
            return {"codes": codes, "plane": plane, "words": words, "scales": scales, "lo": lo}

        def load_codes(op, g0=0, g1=PASSES):
            nc.sync.dma_start(
                out=op["codes"][:, g0:g1, :].bitcast(I32),
                in_=op["words"][g0:g1, :, 2 * op["lo"] : 2 * (op["lo"] + BANK)].rearrange("g p n -> p g n").bitcast(I32),
            )

        def load_scales(op):
            for q in range(4):
                nc.sync.dma_start(
                    out=op["plane"][32 * q : 32 * q + 4, :, :].bitcast(I32),
                    in_=op["scales"][:, 4 * q : 4 * q + 4, op["lo"] : op["lo"] + BANK]
                    .rearrange("g r n -> r g n")
                    .bitcast(I32),
                )

        def bias_line(line, lo):
            nc.scalar.dma_start(out=line[0:1, :], in_=qkv_b[lo : lo + BANK].rearrange("(o n) -> o n", o=1))

        x_ops = {}
        w_ops = {}
        x_ops[0] = operand("x0", x_words, x_scales, 0, "vector")
        w_ops[0] = operand("w0", qkv_w_words, qkv_w_scales, 0, "gpsimd")
        b_lines = []
        for i in range(3):
            line = keep.tile([P, BANK], BF16, name="b_line%d" % i)
            b_lines.append(line)
        nc.vector.memset(b_lines[0][:], 0.0)
        b_rows = keep.tile([P, P], BF16, name="b_rows")
        nc.vector.memset(b_rows[:], 0.0)
        ones = keep.tile([P, BANK], BF16, name="ones")
        nc.vector.memset(ones[:], 1.0)
        warm = keep.tile([P, 1], F32, name="warm")
        warm_out = keep.tile([P, 1], F32, name="warm_out")
        nc.vector.memset(warm[:], 0.0)
        ident = keep.tile([P, P], F32, name="ident")
        make_identity(nc, ident[:])
        x_ops[1] = operand("x1", x_words, x_scales, TOK, "vector")
        nc.vector.memset(b_lines[1][:], 0.0)
        nc.vector.memset(b_lines[2][:], 0.0)
        for i in W_ORDER[1:]:
            w_ops[i] = operand("w%d" % i, qkv_w_words, qkv_w_scales, i * BANK, "gpsimd")
        cos = keep.tile([P, SLOTS, HD], BF16, name="cos")
        sin = keep.tile([P, SLOTS, HD], BF16, name="sin")
        cos_n = keep.tile([P, SLOTS, HD], BF16, name="cos_n")
        sin_n = keep.tile([P, SLOTS, HD], BF16, name="sin_n")

        bias_line(b_lines[0], 0)
        nc.scalar.dma_start(out=b_rows[0 : 2 * HEADS, :], in_=qkv_b[0:V0].rearrange("(c d) -> c d", d=HD))
        nc.scalar.activation(out=warm_out[:], in_=warm[:], func=ACT.Identity, bias=0.0, scale=1.0)
        bias_line(b_lines[1], V0)
        bias_line(b_lines[2], V0 + BANK)
        load_codes(x_ops[0])
        load_codes(w_ops[0])
        load_scales(x_ops[0])
        load_scales(w_ops[0])
        nc.sync.dma_start(out=cos_n[:], in_=rope_cos[0, 0].rearrange("(t p) d -> p t d", p=P))
        nc.sync.dma_start(out=sin_n[:], in_=rope_sin[0, 0].rearrange("(t p) d -> p t d", p=P))
        load_codes(x_ops[1])
        load_scales(x_ops[1])
        nc.sync.dma_start(out=cos[:], in_=rope_cos[0, 0].rearrange("(p s) d -> p s d", s=SLOTS))
        nc.sync.dma_start(out=sin[:], in_=rope_sin[0, 0].rearrange("(p s) d -> p s d", s=SLOTS))
        for i in W_ORDER[1:]:
            load_codes(w_ops[i])
            load_scales(w_ops[i])

        heat = psum.tile([P, BANK], F32, tag="bank")
        for i in range(WARM):
            nc.tensor.matmul(out=heat[:], lhsT=ones[:, 0:P], rhs=ones[:], start=True, stop=True)

        b_rows_f = keep.tile([P, P], F32, name="b_rows_f")
        nc.vector.tensor_copy(out=b_rows_f[:], in_=b_rows[:])
        b_t = psum.tile([P, P], F32, tag="bank")
        nc.tensor.transpose(out=b_t[:], in_=b_rows_f[:], identity=ident[:])
        b_col = keep.tile([P, 2 * HEADS], F32, name="b_col")
        nc.vector.tensor_copy(out=b_col[:], in_=b_t[:, 0 : 2 * HEADS])
        b_free = keep.tile([P, 3 * BANK], F32, name="b_free")

        def spread_bias(blocks):
            for cb in blocks:
                spread = psum.tile([P, BANK], F32, tag="bank")
                nc.tensor.matmul(
                    out=spread[:], lhsT=ones[:, 0:P], rhs=b_lines[cb][:], start=True, stop=True
                )
                nc.scalar.activation(
                    out=b_free[:, cb * BANK : (cb + 1) * BANK], in_=spread[:], func=ACT.Identity, bias=0.0, scale=1.0
                )

        spread_bias([0])

        def project(acc, l_op, l0, r_op):
            for g in range(PASSES):
                nc.tensor.matmul_mx(
                    out=acc,
                    lhsT=l_op["codes"][:, g, 2 * l0 : 2 * (l0 + P)].bitcast(FP4X4),
                    lhsT_scale=l_op["plane"][:, g, l0 : l0 + P],
                    rhs=r_op["codes"][:, g, :].bitcast(FP4X4),
                    rhs_scale=r_op["plane"][:, g, :],
                    start=(g == 0),
                    stop=(g == PASSES - 1),
                )

        def qk_project(b, jh):
            acc = psum.tile([P, TOK], F32, tag="bank")
            project(acc[:], w_ops[jh * HD // BANK], jh * HD % BANK, x_ops[b])
            u = work.tile([P, SLOTS, P], F32, tag="u", bufs=2 * ROUND)
            nc.scalar.activation(
                out=u[:],
                in_=acc[:].rearrange("c (p s) -> c s p", s=SLOTS),
                func=ACT.Identity,
                bias=b_col[:, jh : jh + 1],
                scale=1.0,
            )
            return u

        def to_tokens(u):
            ut = psum.tile([P, SLOTS, HD], F32, tag="bank")
            for s in range(SLOTS):
                nc.tensor.transpose(out=ut[:, s, :], in_=u[:, s, :], identity=ident[:])
            return ut

        def rope(ut, a, r):
            nc.vector.tensor_tensor(out=a, in0=ut[:], in1=cos[:], op=ALU.mult)
            nc.vector.tensor_tensor(out=r[:, :, 0:HALF], in0=ut[:, :, HALF:HD], in1=sin[:, :, 0:HALF], op=ALU.mult)
            nc.vector.tensor_tensor(out=r[:, :, HALF:HD], in0=ut[:, :, 0:HALF], in1=sin[:, :, HALF:HD], op=ALU.mult)

        def rope_heads(b, heads, uts):
            n = len(heads)
            a2 = work.tile([P, PAIR, SLOTS, HD], F32, tag="a2", bufs=6)
            r2 = work.tile([P, PAIR, SLOTS, HD], F32, tag="r2", bufs=6)
            o2 = work.tile([P, PAIR, SLOTS, HD], F32, tag="o2", bufs=4)
            for i in range(n):
                rope(uts[i], a2[:, i], r2[:, i])
            nc.gpsimd.tensor_tensor(
                out=o2[:, 0:n].rearrange("p u s d -> p (u s d)"),
                in0=a2[:, 0:n].rearrange("p u s d -> p (u s d)"),
                in1=r2[:, 0:n].rearrange("p u s d -> p (u s d)"),
                op=ALU.add,
            )
            dst = out_0 if heads[0] < HEADS else out_1
            h = heads[0] % HEADS
            return (
                dst[b, h : h + n].rearrange("u (p s) d -> p u (s d)", s=SLOTS),
                o2[:, 0:n].rearrange("p u s d -> p u (s d)"),
            )

        def v_project(tb, cb):
            acc = psum.tile([P, BANK], F32, tag="bank")
            project(acc[:], x_ops[tb // 4], (tb % 4) * P, w_ops[4 + cb])
            return acc

        def v_finish(acc, tb, cb, queue):
            o = work.tile([P, 4, HD], F32, tag="ov", bufs=8)
            nc.vector.tensor_tensor(
                out=o[:].rearrange("p h d -> p (h d)"), in0=acc[:], in1=b_free[:, (1 + cb) * BANK : (2 + cb) * BANK], op=ALU.add
            )
            t0 = (tb % 4) * P
            queue.dma_start(
                out=out_2[tb // 4, 4 * cb : 4 * cb + 4, t0 : t0 + P, :].rearrange("h p d -> p h d"), in_=o[:]
            )

        def direct_project(t):
            acc = psum.tile([P, BANK], F32, tag="bank")
            project(acc[:], x_ops[0], t * P, w_ops[0])
            u = work.tile([P, 4, HD], F32, tag="ud", bufs=4)
            nc.vector.tensor_tensor(out=u[:].rearrange("p h d -> p (h d)"), in0=acc[:], in1=b_free[:, 0:BANK], op=ALU.add)
            return u

        def direct_rope(u, t, a, r):
            nc.vector.tensor_tensor(out=a, in0=u[:], in1=cos_n[:, t : t + 1, :].to_broadcast([P, 4, HD]), op=ALU.mult)
            nc.vector.tensor_tensor(
                out=r[:, :, 0:HALF],
                in0=u[:, :, HALF:HD],
                in1=sin_n[:, t : t + 1, 0:HALF].to_broadcast([P, 4, HALF]),
                op=ALU.mult,
            )
            nc.vector.tensor_tensor(
                out=r[:, :, HALF:HD],
                in0=u[:, :, 0:HALF],
                in1=sin_n[:, t : t + 1, HALF:HD].to_broadcast([P, 4, HALF]),
                op=ALU.mult,
            )

        a4 = work.tile([P, SLOTS, 4, HD], F32, tag="a4", bufs=1)
        r4 = work.tile([P, SLOTS, 4, HD], F32, tag="r4", bufs=1)
        o4 = work.tile([P, SLOTS, 4, HD], F32, tag="o4", bufs=1)
        uds = []
        for t in range(SLOTS + 1):
            if t < SLOTS:
                uds.append(direct_project(t))
            if t == 1:
                nc.vector.tensor_scalar_mul(out=sin_n[:, :, 0:HALF], in0=sin_n[:, :, 0:HALF], scalar1=-1.0)
            if t > 0:
                direct_rope(uds[t - 1], t - 1, a4[:, t - 1], r4[:, t - 1])
        nc.gpsimd.tensor_tensor(
            out=o4[:].rearrange("p t h d -> p (t h d)"),
            in0=a4[:].rearrange("p t h d -> p (t h d)"),
            in1=r4[:].rearrange("p t h d -> p (t h d)"),
            op=ALU.add,
        )
        for t in range(SLOTS):
            nc.sync.dma_start(out=out_0[0, 0:4, t * P : (t + 1) * P, :].rearrange("h p d -> p h d"), in_=o4[:, t])

        nc.vector.tensor_scalar_mul(out=sin[:, :, 0:HALF], in0=sin[:, :, 0:HALF], scalar1=-1.0)
        units = [(b, 4 * c + i) for c in range(2 * HEADS // 4) for b in range(BATCH) for i in range(4)][4:]
        rounds = []
        for size in ROUND_SIZES:
            rounds.append((units[0][0], [jh for b, jh in units[0:size]]))
            units = units[size:]
        v_units = [(tb, cb) for cb in range(2) for tb in range(8)]

        for r in range(len(rounds) - 1):
            b, heads = rounds[r]
            us = [qk_project(b, jh) for jh in heads]
            if r == 0:
                spread_bias([1, 2])
            uts = [to_tokens(u) for u in us]
            v_accs = []
            for i in range(V_PER_ROUND[r]):
                unit = v_units.pop(0)
                v_accs.append((v_project(*unit), unit))
            for i0 in range(0, len(heads), PAIR):
                dst_ap, src_ap = rope_heads(b, heads[i0 : i0 + PAIR], uts[i0 : i0 + PAIR])
                for i in range(1 if i0 + PAIR < len(heads) else len(v_accs)):
                    if v_accs:
                        acc, unit = v_accs.pop(0)
                        v_finish(acc, unit[0], unit[1], nc.sync)
                nc.sync.dma_start(out=dst_ap, in_=src_ap)

        b, heads = rounds[-1]
        us = [qk_project(b, jh) for jh in heads]
        uts = [to_tokens(u) for u in us]
        state = {"live": len(heads)}
        v_accs = []

        def fill_banks():
            while v_units and state["live"] < BANKS:
                unit = v_units.pop(0)
                v_accs.append((v_project(*unit), unit))
                state["live"] += 1

        def finish_v(n):
            for i in range(n):
                if v_accs:
                    acc, unit = v_accs.pop(0)
                    v_finish(acc, unit[0], unit[1], nc.scalar)
                    state["live"] -= 1
                    fill_banks()

        fill_banks()
        for i in range(len(heads)):
            dst_ap, src_ap = rope_heads(b, heads[i : i + 1], uts[i : i + 1])
            nc.sync.dma_start(out=dst_ap, in_=src_ap)
            state["live"] -= 1
            fill_banks()
            if i > 0:
                finish_v(END_V)
        finish_v(len(v_units) + len(v_accs))
